import numpy as np
import ml_dtypes


def mxq(x, axis, fmt="e4m3"):
    dtype, down = {"e4m3": (ml_dtypes.float8_e4m3fn, 7), "e5m2": (ml_dtypes.float8_e5m2, 14)}[fmt]
    v = np.moveaxis(np.asarray(x, np.float32).astype(ml_dtypes.bfloat16).astype(np.float64), axis, -1)
    blocks = v.reshape(v.shape[:-1] + (-1, 32))
    amax = np.abs(blocks).max(-1, keepdims=True)
    byte = np.maximum(np.where(amax > 0, np.frexp(amax)[1] - 1 + 127, 0) - down, 1)
    scale = np.exp2(byte - 127.0)
    codes = (blocks / scale).astype(np.float32).astype(dtype).astype(np.float64)
    return np.moveaxis((codes * scale).reshape(v.shape), -1, axis)


WIDE = False


def mx_kscale(k):
    if not WIDE:
        return np.ones(k)
    levels = np.array([10, -10, 5, -5, 0])
    if k % 512:
        return np.exp2(np.random.permutation(np.resize(levels, k // 32))).repeat(32)
    a = np.empty((k // 512, 16))
    for p in range(k // 512):
        a[p, :8] = np.random.permutation(np.resize(levels, 8))
        for g in range(8):
            far = levels[np.abs(levels - a[p, g]) >= 10]
            a[p, g + 8] = far[np.random.randint(len(far))]
    return np.exp2(a.ravel()).repeat(32)


BF16 = ml_dtypes.bfloat16


def bf(x):
    return np.asarray(x, np.float32).astype(BF16)


def f64(x):
    return np.asarray(x).astype(np.float64)


B, Q, K, D = 2, 512, 1024, 1024
NEG = -10000.0


def setup_inputs():
    s, t = mx_kscale(D), mx_kscale(D)
    return {"query": bf(np.random.standard_normal((B, Q, D)) * s),
            "context": bf(np.random.standard_normal((B, K, D)) * 0.5 / t),
            "query_bit": bf(np.random.random((B, Q)) > 0.25),
            "context_bit": bf(np.random.random((B, K)) > 0.25),
            "W_in": bf(np.random.standard_normal((D, D)) * 4.0 / D * t[:, None] / s[None, :]),
            "b_in": bf(np.random.standard_normal(D) / np.sqrt(D) * t)}


def reference(query, context, query_bit, context_bit, W_in, b_in):
    ext = (1.0 - f64(query_bit)[:, :, None] * f64(context_bit)[:, None, :]) * NEG
    q = (mxq(f64(query), 2, "e4m3") @ mxq(f64(W_in), 1, "e4m3").T) + f64(b_in)
    scores = (mxq(q, 2, "e4m3") @ mxq(f64(context), 2, "e4m3").transpose(0, 2, 1)) + ext
    e = np.exp(scores - scores.max(-1, keepdims=True))
    return e / e.sum(-1, keepdims=True)

@@ -1,0 +1,343 @@
+from contextlib import ExitStack
+
+import concourse.mybir as mybir
+from concourse.masks import make_identity
+
+F32 = mybir.dt.float32
+BF16 = mybir.dt.bfloat16
+U32 = mybir.dt.uint32
+U8 = mybir.dt.uint8
+FP8X4 = mybir.dt.float8_e4m3fn_x4
+ALU = mybir.AluOpType
+ACT = mybir.ActivationFunctionType
+AX = mybir.AxisListType
+
+P = 128
+BANK = 512
+FEATURES = 1024
+CONTEXT_ROWS = 1024
+MASKED = 10000.0
+
+GROUPS = ["q0", "w0", "w1", "c00", "c01", "q1", "c10", "c11"]
+
+FLOPS = 2 * 1024 * 1024 * 1024 + 2 * 2 * 512 * 1024 * 1024
+
+
+def tile_attention_pa_kernel(tc, query, context, query_bit, context_bit, W_in, b_in, out):
+    nc = tc.nc
+    with ExitStack() as ctx:
+        const = ctx.enter_context(tc.tile_pool(name="const", bufs=1))
+        loaded = ctx.enter_context(tc.tile_pool(name="loaded", bufs=1))
+        packed = ctx.enter_context(tc.tile_pool(name="packed", bufs=1))
+        staging = ctx.enter_context(tc.tile_pool(name="staging", bufs=8))
+        soft = ctx.enter_context(tc.tile_pool(name="soft", bufs=8))
+        stats = ctx.enter_context(tc.tile_pool(name="stats", bufs=8))
+        turned = ctx.enter_context(tc.psum_pool(name="turned", bufs=4))
+        sums = ctx.enter_context(tc.psum_pool(name="sums", bufs=4))
+        ctx.enter_context(tc.manual_schedule())
+
+        warm = const.tile([P, 2], F32, name="warm")
+        nc.vector.memset(warm[:], 0.0)
+        nc.scalar.activation(out=warm[:, 1:2], in_=warm[:, 0:1], func=ACT.Exp)
+
+        mask_rows = const.tile([P, 2 * CONTEXT_ROWS], BF16, name="mask_rows")
+        nc.vector.memset(mask_rows[:], 0.0)
+        ones = const.tile([P, P], BF16, name="ones")
+        nc.vector.memset(ones[:], 1.0)
+        identity = const.tile([P, P], F32, name="identity")
+        make_identity(nc, identity[:])
+        bits_row = const.tile([1, 2 * CONTEXT_ROWS], BF16, name="bits_row")
+        mask = const.tile([P, 2 * CONTEXT_ROWS], BF16, name="mask")
+        bias_bf16 = const.tile([P, 8], BF16, name="bias_bf16")
+        bias = const.tile([P, 8], F32, name="bias")
+        query_bits = const.tile([P, 8], BF16, name="query_bits")
+        penalty = const.tile([P, 8], F32, name="penalty")
+
+        raw = {}
+        grouped = {}
+        codes = {}
+        scales = {}
+        mask_bank = {}
+        q_planes = {}
+        q_grouped = {}
+        q_words = {}
+        score = {}
+        negative_max = {}
+        row_sum = {}
+        inverse_sum = {}
+
+        def load(group, half):
+            if half == 0:
+                raw[group] = loaded.tile([P, 4 * FEATURES], BF16, name="raw_" + group)
+            if group[0] == "q":
+                rows = query[int(group[1])].rearrange("(p n) d -> p n d", n=4)[:, 2 * half : 2 * half + 2, :]
+            elif group[0] == "w":
+                first = 512 * int(group[1])
+                rows = W_in[first : first + 512, :].rearrange("(p t) d -> p t d", t=4)
+                rows = rows[:, 2 * half : 2 * half + 2, :]
+            else:
+                first = 512 * int(group[2])
+                rows = context[int(group[1]), first : first + 512, :].rearrange("(p c) e -> p c e", c=4)
+                rows = rows[:, 2 * half : 2 * half + 2, :]
+            nc.sync.dma_start(
+                out=raw[group][:, 2 * FEATURES * half : 2 * FEATURES * (half + 1)].rearrange("p (n k) -> p n k", n=2),
+                in_=rows,
+            )
+
+        def prepare(group, half, vector_helps):
+            words = raw[group][:].bitcast(F32)
+            for k_pass in range(2):
+                if half == 0:
+                    grouped[(group, k_pass)] = staging.tile([P, 4 * BANK], BF16, name="grouped", align_bytes=64)
+                bank = turned.tile([P, BANK], F32, name="bank")
+                for a in range(2):
+                    for u in range(2):
+                        first = 512 * (2 * half + a) + 256 * k_pass
+                        nc.tensor.transpose(
+                            bank[:, (2 * a + u) * P : (2 * a + u + 1) * P],
+                            words[:, first + u : first + 2 * P : 2],
+                            identity[:],
+                        )
+                target = grouped[(group, k_pass)][:].bitcast(F32)[:, BANK * half : BANK * (half + 1)]
+                target = target.rearrange("p (a r u) -> p a r u", a=2, u=2)
+                source = bank[:].rearrange("p (a u r) -> p a r u", a=2, u=2)
+                if vector_helps and k_pass == 1:
+                    nc.vector.tensor_copy(out=target, in_=source)
+                else:
+                    nc.scalar.copy(out=target, in_=source)
+
+        def quantise(operand, values):
+            width = values.shape[1] // 4
+            codes[operand] = packed.tile([P, width], U32, name="codes_%s_%d_%d" % operand, align_bytes=64)
+            scales[operand] = packed.tile([P, width], U8, name="scales_%s_%d_%d" % operand, align_bytes=64)
+            nc.vector.quantize_mx(out=codes[operand][:].bitcast(FP8X4), scales=scales[operand][:], in_=values)
+
+        def quantise_group(group):
+            for k_pass in range(2):
+                quantise((group, k_pass, 0), grouped[(group, k_pass)][:])
+
+        def multiply(acc, stationary, stationary_columns, moving, moving_columns, k_pass):
+            nc.tensor.matmul_mx(
+                out=acc,
+                lhsT=codes[stationary][:, stationary_columns].bitcast(FP8X4),
+                lhsT_scale=scales[stationary][:, stationary_columns],
+                rhs=codes[moving][:, moving_columns].bitcast(FP8X4),
+                rhs_scale=scales[moving][:, moving_columns],
+                start=(k_pass == 0),
+                stop=(k_pass == 1),
+            )
+
+        def make_mask_row():
+            nc.vector.tensor_scalar(out=mask_rows[0:1, :], in0=bits_row[:], scalar1=-1.0, scalar2=None, op0=ALU.add)
+
+        def spread_mask():
+            for b in range(2):
+                mask_bank[b] = sums.tile([P, CONTEXT_ROWS], BF16, name="mask_bank", tag="acc")
+                for h in range(2):
+                    first = CONTEXT_ROWS * b + BANK * h
+                    nc.tensor.matmul(
+                        out=mask_bank[b][:, BANK * h : BANK * (h + 1)],
+                        lhsT=ones[:],
+                        rhs=mask_rows[:, first : first + BANK],
+                        start=True,
+                        stop=True,
+                    )
+
+        def copy_mask(b, on_vector):
+            target = mask[:, CONTEXT_ROWS * b : CONTEXT_ROWS * (b + 1)]
+            if on_vector:
+                nc.vector.tensor_copy(out=target, in_=mask_bank[b][:])
+            else:
+                nc.scalar.copy(out=target, in_=mask_bank[b][:])
+
+        def project_on_vector(b, e_pass, half):
+            if half == 0:
+                q_grouped[(b, e_pass)] = staging.tile([P, 4 * BANK], BF16, name="q_grouped", bufs=4, align_bytes=64)
+            query_tiles = (2 * half, 2 * half + 1)
+            acc = {}
+            for n in query_tiles:
+                acc[n] = sums.tile([P, BANK], F32, name="acc")
+                for t in range(4):
+                    for d_pass in range(2):
+                        multiply(
+                            acc[n][:, P * t : P * (t + 1)],
+                            ("w%d" % e_pass, d_pass, 0), slice(P * t, P * (t + 1)),
+                            ("q%d" % b, d_pass, 0), slice(P * n, P * (n + 1)),
+                            d_pass,
+                        )
+            for n in query_tiles:
+                nc.vector.tensor_tensor(
+                    out=q_grouped[(b, e_pass)][:, BANK * n : BANK * (n + 1)].rearrange("p (i t) -> p i t", t=4),
+                    in0=acc[n][:].rearrange("p (t i) -> p i t", t=4),
+                    in1=bias[:, 4 * e_pass : 4 * e_pass + 4].unsqueeze(1).to_broadcast([P, P, 4]),
+                    op=ALU.add,
+                )
+            for n in query_tiles:
+                quantise(("z%d" % b, e_pass, n), q_grouped[(b, e_pass)][:, BANK * n : BANK * (n + 1)])
+                q_words[(b, e_pass, n)] = (("z%d" % b, e_pass, n), slice(0, P))
+
+        def project_on_scalar(b, e_pass):
+            q_planes[(b, e_pass)] = staging.tile([P, 4 * BANK], BF16, name="q_planes", bufs=2)
+            q_grouped[(b, e_pass)] = staging.tile([P, 4 * BANK], BF16, name="q_grouped", bufs=4, align_bytes=64)
+            for t in range(4):
+                acc = sums.tile([P, BANK], F32, name="acc")
+                for d_pass in range(2):
+                    multiply(
+                        acc[:],
+                        ("w%d" % e_pass, d_pass, 0), slice(P * t, P * (t + 1)),
+                        ("q%d" % b, d_pass, 0), slice(0, BANK),
+                        d_pass,
+                    )
+                nc.scalar.activation(
+                    out=q_planes[(b, e_pass)][:, BANK * t : BANK * (t + 1)],
+                    in_=acc[:],
+                    func=ACT.Identity,
+                    bias=bias[:, 4 * e_pass + t : 4 * e_pass + t + 1],
+                    scale=1.0,
+                )
+            planes = q_planes[(b, e_pass)][:].rearrange("p (t i) -> p t i", t=4)
+            for half in range(2):
+                target = q_grouped[(b, e_pass)][:, 2 * BANK * half : 2 * BANK * (half + 1)]
+                nc.gpsimd.tensor_scalar(
+                    out=target.rearrange("p (m f t) -> p m t f", f=4, t=4),
+                    in0=planes[:, :, 2 * P * half : 2 * P * (half + 1)].rearrange("p t (m f) -> p m t f", f=4),
+                    scalar1=1.0,
+                    scalar2=0.0,
+                    op0=ALU.mult,
+                    op1=ALU.add,
+                )
+
+        def quantise_q(b, e_pass):
+            for half in range(2):
+                operand = ("z%d" % b, e_pass, half)
+                quantise(operand, q_grouped[(b, e_pass)][:, 2 * BANK * half : 2 * BANK * (half + 1)])
+                for a in range(2):
+                    q_words[(b, e_pass, 2 * half + a)] = (operand, slice(P * a, P * (a + 1)))
+
+        def scores(b, n):
+            score[(b, n)] = soft.tile([P, CONTEXT_ROWS], F32, name="score")
+            for h in range(2):
+                acc = sums.tile([P, BANK], F32, name="acc")
+                for e_pass in range(2):
+                    operand, columns = q_words[(b, e_pass, n)]
+                    multiply(acc[:], operand, columns, ("c%d%d" % (b, h), e_pass, 0), slice(0, BANK), e_pass)
+                first = CONTEXT_ROWS * b + BANK * h
+                nc.vector.scalar_tensor_tensor(
+                    out=score[(b, n)][:, BANK * h : BANK * (h + 1)].rearrange("p (r c) -> p r c", c=4),
+                    in0=mask[:, first : first + BANK].rearrange("p (r c) -> p r c", c=4),
+                    scalar=penalty[:, 4 * b + n : 4 * b + n + 1],
+                    in1=acc[:].rearrange("p (c r) -> p r c", c=4),
+                    op0=ALU.mult,
+                    op1=ALU.add,
+                )
+            negative_max[(b, n)] = stats.tile([P, 1], F32, name="negative_max")
+            nc.vector.tensor_reduce(
+                out=negative_max[(b, n)][:], in_=score[(b, n)][:], axis=AX.X, op=ALU.max, negate=True
+            )
+
+        def exponentials(b, n):
+            row_sum[(b, n)] = stats.tile([P, 1], F32, name="row_sum")
+            nc.scalar.activation(
+                out=score[(b, n)][:],
+                in_=score[(b, n)][:],
+                func=ACT.Exp,
+                bias=negative_max[(b, n)][:],
+                scale=1.0,
+                accum_out=row_sum[(b, n)][:],
+            )
+
+        def reciprocal(b, n):
+            inverse_sum[(b, n)] = stats.tile([P, 1], F32, name="inverse_sum")
+            nc.vector.reciprocal(inverse_sum[(b, n)][:], row_sum[(b, n)][:])
+
+        def normalise_and_store(b, n, on_vector):
+            weights = score[(b, n)]
+            if on_vector:
+                nc.vector.tensor_scalar(
+                    out=weights[:], in0=weights[:], scalar1=inverse_sum[(b, n)][:], scalar2=None, op0=ALU.mult
+                )
+            else:
+                nc.gpsimd.tensor_scalar(
+                    out=weights[:], in0=weights[:], scalar1=inverse_sum[(b, n)][:], scalar2=0.0,
+                    op0=ALU.mult, op1=ALU.add,
+                )
+            nc.sync.dma_start(out=out[b].rearrange("(p n) j -> p n j", n=4)[:, n, :], in_=weights[:])
+
+        for group in GROUPS:
+            for half in range(2):
+                load(group, half)
+                if (group, half) == ("q0", 0):
+                    nc.sync.dma_start(out=bits_row[:], in_=context_bit.rearrange("(o b) j -> o (b j)", o=1))
+                if (group, half) == ("w0", 1):
+                    nc.sync.dma_start(
+                        out=bias_bf16[:].rearrange("p (g t) -> p g t", g=2),
+                        in_=b_in.rearrange("(g p t) -> p g t", g=2, t=4),
+                    )
+                    nc.sync.dma_start(
+                        out=query_bits[:].rearrange("p (b n) -> p b n", b=2),
+                        in_=query_bit.rearrange("b (p n) -> p b n", n=4),
+                    )
+
+        make_mask_row()
+        prepare("q0", 0, True)
+        prepare("q0", 1, True)
+        spread_mask()
+        quantise_group("q0")
+        copy_mask(0, True)
+        prepare("w0", 0, True)
+        prepare("w0", 1, False)
+        quantise_group("w0")
+        prepare("w1", 0, True)
+        prepare("w1", 1, True)
+        quantise_group("w1")
+        copy_mask(1, False)
+        nc.vector.tensor_copy(out=bias[:], in_=bias_bf16[:])
+
+        project_on_vector(0, 0, 0)
+        project_on_vector(0, 0, 1)
+        prepare("c00", 0, False)
+        prepare("c00", 1, False)
+        project_on_vector(0, 1, 0)
+        quantise_group("c00")
+        prepare("c01", 0, False)
+        prepare("c01", 1, False)
+        project_on_vector(0, 1, 1)
+        quantise_group("c01")
+        prepare("q1", 0, False)
+        prepare("q1", 1, False)
+        prepare("c10", 0, False)
+        quantise_group("q1")
+        nc.vector.tensor_scalar(out=penalty[:], in0=query_bits[:], scalar1=MASKED, scalar2=None, op0=ALU.mult)
+
+        scores(0, 0)
+        prepare("c10", 1, False)
+        scores(0, 1)
+        quantise_group("c10")
+        project_on_scalar(1, 0)
+        exponentials(0, 0)
+        scores(0, 2)
+        quantise_q(1, 0)
+        reciprocal(0, 0)
+        project_on_scalar(1, 1)
+        exponentials(0, 1)
+        scores(0, 3)
+        reciprocal(0, 1)
+        quantise_q(1, 1)
+        prepare("c11", 0, False)
+        prepare("c11", 1, False)
+        quantise_group("c11")
+        exponentials(0, 2)
+        exponentials(0, 3)
+        reciprocal(0, 2)
+        for n in range(3):
+            normalise_and_store(0, n, False)
+
+        before = (0, 3)
+        for n in range(4):
+            scores(1, n)
+            reciprocal(before[0], before[1])
+            normalise_and_store(before[0], before[1], n == 3)
+            exponentials(1, n)
+            before = (1, n)
+        reciprocal(before[0], before[1])
+        normalise_and_store(before[0], before[1], True)

@@ -44,6 +44,8 @@ def tile_attention_pa_kernel(tc, query, context, query_bit, context_bit, W_in, b
         nc.vector.memset(mask_rows[:], 0.0)
         ones = const.tile([P, P], BF16, name="ones")
         nc.vector.memset(ones[:], 1.0)
+        blank = const.tile([P, BANK], BF16, name="blank")
+        nc.vector.memset(blank[:], 0.0)
         identity = const.tile([P, P], F32, name="identity")
         make_identity(nc, identity[:])
         bits_row = const.tile([1, 2 * CONTEXT_ROWS], BF16, name="bits_row")
@@ -83,6 +85,13 @@ def tile_attention_pa_kernel(tc, query, context, query_bit, context_bit, W_in, b
                 out=raw[group][:, 2 * FEATURES * half : 2 * FEATURES * (half + 1)].rearrange("p (n k) -> p n k", n=2),
                 in_=rows,
             )
+
+        def keep_warm(columns, count):
+            unread = sums.tile([P, BANK], F32, name="unread", tag="acc")
+            for repeat in range(count):
+                nc.tensor.matmul(
+                    out=unread[:, 0:columns], lhsT=blank[:, 0:P], rhs=blank[:, 0:columns], start=True, stop=True
+                )
 
         def prepare(group, half, vector_helps):
             words = raw[group][:].bitcast(F32)
@@ -279,15 +288,19 @@ def tile_attention_pa_kernel(tc, query, context, query_bit, context_bit, W_in, b
                     )
 
         make_mask_row()
+        keep_warm(BANK, 6)
         prepare("q0", 0, True)
         prepare("q0", 1, True)
         spread_mask()
         quantise_group("q0")
         copy_mask(0, True)
         prepare("w0", 0, True)
+        keep_warm(BANK // 2, 1)
         prepare("w0", 1, False)
+        keep_warm(BANK // 2, 1)
         quantise_group("w0")
         prepare("w1", 0, True)
+        keep_warm(BANK // 2, 1)
         prepare("w1", 1, True)
         quantise_group("w1")
         copy_mask(1, False)
@@ -296,15 +309,19 @@ def tile_attention_pa_kernel(tc, query, context, query_bit, context_bit, W_in, b
         project_on_vector(0, 0, 0)
         project_on_vector(0, 0, 1)
         prepare("c00", 0, False)
+        keep_warm(BANK // 2, 1)
         prepare("c00", 1, False)
         project_on_vector(0, 1, 0)
         quantise_group("c00")
         prepare("c01", 0, False)
+        keep_warm(BANK // 2, 1)
         prepare("c01", 1, False)
         project_on_vector(0, 1, 1)
         quantise_group("c01")
         prepare("q1", 0, False)
+        keep_warm(BANK // 2, 1)
         prepare("q1", 1, False)
+        keep_warm(BANK // 2, 1)
         prepare("c10", 0, False)
         quantise_group("q1")
         nc.vector.tensor_scalar(out=penalty[:], in0=query_bits[:], scalar1=MASKED, scalar2=None, op0=ALU.mult)
@@ -324,6 +341,7 @@ def tile_attention_pa_kernel(tc, query, context, query_bit, context_bit, W_in, b
         reciprocal(0, 1)
         quantise_q(1, 1)
         prepare("c11", 0, False)
+        keep_warm(BANK // 2, 1)
         prepare("c11", 1, False)
         quantise_group("c11")
         exponentials(0, 2)

@@ -36,16 +36,17 @@ def tile_attention_pa_kernel(tc, query, context, query_bit, context_bit, W_in, b
         sums = ctx.enter_context(tc.psum_pool(name="sums", bufs=4))
         ctx.enter_context(tc.manual_schedule())
 
+        blank = const.tile([P, BANK], BF16, name="blank")
+        nc.vector.memset(blank[:].bitcast(U32), 0)
+
         warm = const.tile([P, 2], F32, name="warm")
         nc.vector.memset(warm[:], 0.0)
         nc.scalar.activation(out=warm[:, 1:2], in_=warm[:, 0:1], func=ACT.Exp)
 
         mask_rows = const.tile([P, 2 * CONTEXT_ROWS], BF16, name="mask_rows")
-        nc.vector.memset(mask_rows[:], 0.0)
+        nc.vector.memset(mask_rows[:].bitcast(U32), 0)
         ones = const.tile([P, P], BF16, name="ones")
         nc.vector.memset(ones[:], 1.0)
-        blank = const.tile([P, BANK], BF16, name="blank")
-        nc.vector.memset(blank[:], 0.0)
         identity = const.tile([P, P], F32, name="identity")
         make_identity(nc, identity[:])
         bits_row = const.tile([1, 2 * CONTEXT_ROWS], BF16, name="bits_row")

@@ -224,9 +224,11 @@ def tile_attention_pa_kernel(tc, query, context, query_bit, context_bit, W_in, b
                 for a in range(2):
                     q_words[(b, e_pass, 2 * half + a)] = (operand, slice(P * a, P * (a + 1)))
 
-        def scores(b, n):
+        def scores(b, n, before):
             score[(b, n)] = soft.tile([P, CONTEXT_ROWS], F32, name="score")
             for h in range(2):
+                if h == 1 and before is not None:
+                    row_maximum(before[0], before[1])
                 acc = sums.tile([P, BANK], F32, name="acc")
                 for e_pass in range(2):
                     operand, columns = q_words[(b, e_pass, n)]
@@ -240,6 +242,8 @@ def tile_attention_pa_kernel(tc, query, context, query_bit, context_bit, W_in, b
                     op0=ALU.mult,
                     op1=ALU.add,
                 )
+
+        def row_maximum(b, n):
             negative_max[(b, n)] = stats.tile([P, 1], F32, name="negative_max")
             nc.vector.tensor_reduce(
                 out=negative_max[(b, n)][:], in_=score[(b, n)][:], axis=AX.X, op=ALU.max, negate=True
@@ -260,18 +264,19 @@ def tile_attention_pa_kernel(tc, query, context, query_bit, context_bit, W_in, b
             inverse_sum[(b, n)] = stats.tile([P, 1], F32, name="inverse_sum")
             nc.vector.reciprocal(inverse_sum[(b, n)][:], row_sum[(b, n)][:])
 
-        def normalise_and_store(b, n, on_vector):
-            weights = score[(b, n)]
-            if on_vector:
-                nc.vector.tensor_scalar(
-                    out=weights[:], in0=weights[:], scalar1=inverse_sum[(b, n)][:], scalar2=None, op0=ALU.mult
-                )
-            else:
-                nc.gpsimd.tensor_scalar(
-                    out=weights[:], in0=weights[:], scalar1=inverse_sum[(b, n)][:], scalar2=0.0,
-                    op0=ALU.mult, op1=ALU.add,
-                )
-            nc.sync.dma_start(out=out[b].rearrange("(p n) j -> p n j", n=4)[:, n, :], in_=weights[:])
+        def normalise_and_store(b, n, on_vector, pieces=1):
+            width = CONTEXT_ROWS // pieces
+            for piece in range(pieces):
+                weights = score[(b, n)][:, width * piece : width * (piece + 1)]
+                inverse = inverse_sum[(b, n)][:]
+                if on_vector:
+                    nc.vector.tensor_scalar(out=weights, in0=weights, scalar1=inverse, scalar2=None, op0=ALU.mult)
+                else:
+                    nc.gpsimd.tensor_scalar(
+                        out=weights, in0=weights, scalar1=inverse, scalar2=0.0, op0=ALU.mult, op1=ALU.add
+                    )
+                target = out[b].rearrange("(p n) j -> p n j", n=4)[:, n, width * piece : width * (piece + 1)]
+                nc.sync.dma_start(out=target, in_=weights)
 
         for group in GROUPS:
             for half in range(2):
@@ -327,18 +332,22 @@ def tile_attention_pa_kernel(tc, query, context, query_bit, context_bit, W_in, b
         quantise_group("q1")
         nc.vector.tensor_scalar(out=penalty[:], in0=query_bits[:], scalar1=MASKED, scalar2=None, op0=ALU.mult)
 
-        scores(0, 0)
+        scores(0, 0, None)
+        row_maximum(0, 0)
         prepare("c10", 1, False)
-        scores(0, 1)
+        scores(0, 1, None)
+        row_maximum(0, 1)
         quantise_group("c10")
         project_on_scalar(1, 0)
         exponentials(0, 0)
-        scores(0, 2)
+        scores(0, 2, None)
+        row_maximum(0, 2)
         quantise_q(1, 0)
         reciprocal(0, 0)
         project_on_scalar(1, 1)
         exponentials(0, 1)
-        scores(0, 3)
+        scores(0, 3, None)
+        row_maximum(0, 3)
         reciprocal(0, 1)
         quantise_q(1, 1)
         prepare("c11", 0, False)
@@ -352,11 +361,15 @@ def tile_attention_pa_kernel(tc, query, context, query_bit, context_bit, W_in, b
             normalise_and_store(0, n, False)
 
         before = (0, 3)
+        scores(1, 0, None)
         for n in range(4):
-            scores(1, n)
+            if n < 3:
+                scores(1, n + 1, (1, n))
+            else:
+                row_maximum(1, 3)
+            exponentials(1, n)
             reciprocal(before[0], before[1])
             normalise_and_store(before[0], before[1], n == 3)
-            exponentials(1, n)
             before = (1, n)
         reciprocal(before[0], before[1])
-        normalise_and_store(before[0], before[1], True)
+        normalise_and_store(before[0], before[1], True, 2)

from contextlib import ExitStack

import concourse.mybir as mybir
from concourse.masks import make_identity

F32 = mybir.dt.float32
BF16 = mybir.dt.bfloat16
U32 = mybir.dt.uint32
U8 = mybir.dt.uint8
FP8X4 = mybir.dt.float8_e4m3fn_x4
ALU = mybir.AluOpType
ACT = mybir.ActivationFunctionType
AX = mybir.AxisListType

P = 128
BANK = 512
FEATURES = 1024
CONTEXT_ROWS = 1024
MASKED = 10000.0

GROUPS = ["q0", "w0", "w1", "c00", "c01", "q1", "c10", "c11"]

FLOPS = 2 * 1024 * 1024 * 1024 + 2 * 2 * 512 * 1024 * 1024


def tile_attention_pa_kernel(tc, query, context, query_bit, context_bit, W_in, b_in, out):
    nc = tc.nc
    with ExitStack() as ctx:
        const = ctx.enter_context(tc.tile_pool(name="const", bufs=1))
        loaded = ctx.enter_context(tc.tile_pool(name="loaded", bufs=1))
        packed = ctx.enter_context(tc.tile_pool(name="packed", bufs=1))
        staging = ctx.enter_context(tc.tile_pool(name="staging", bufs=8))
        soft = ctx.enter_context(tc.tile_pool(name="soft", bufs=8))
        stats = ctx.enter_context(tc.tile_pool(name="stats", bufs=8))
        turned = ctx.enter_context(tc.psum_pool(name="turned", bufs=4))
        sums = ctx.enter_context(tc.psum_pool(name="sums", bufs=4))
        ctx.enter_context(tc.manual_schedule())

        blank = const.tile([P, BANK], BF16, name="blank")
        nc.vector.memset(blank[:].bitcast(U32), 0)

        warm = const.tile([P, 2], F32, name="warm")
        nc.vector.memset(warm[:], 0.0)
        nc.scalar.activation(out=warm[:, 1:2], in_=warm[:, 0:1], func=ACT.Exp)

        mask_rows = const.tile([P, 2 * CONTEXT_ROWS], BF16, name="mask_rows")
        nc.vector.memset(mask_rows[:].bitcast(U32), 0)
        ones = const.tile([P, P], BF16, name="ones")
        nc.vector.memset(ones[:], 1.0)
        identity = const.tile([P, P], F32, name="identity")
        make_identity(nc, identity[:])
        bits_row = const.tile([1, 2 * CONTEXT_ROWS], BF16, name="bits_row")
        mask = const.tile([P, 2 * CONTEXT_ROWS], BF16, name="mask")
        bias_bf16 = const.tile([P, 8], BF16, name="bias_bf16")
        bias = const.tile([P, 8], F32, name="bias")
        query_bits = const.tile([P, 8], BF16, name="query_bits")
        penalty = const.tile([P, 8], F32, name="penalty")

        raw = {}
        grouped = {}
        codes = {}
        scales = {}
        mask_bank = {}
        q_planes = {}
        q_grouped = {}
        q_words = {}
        score = {}
        negative_max = {}
        row_sum = {}
        inverse_sum = {}

        def load(group, half):
            if half == 0:
                raw[group] = loaded.tile([P, 4 * FEATURES], BF16, name="raw_" + group)
            if group[0] == "q":
                rows = query[int(group[1])].rearrange("(p n) d -> p n d", n=4)[:, 2 * half : 2 * half + 2, :]
            elif group[0] == "w":
                first = 512 * int(group[1])
                rows = W_in[first : first + 512, :].rearrange("(p t) d -> p t d", t=4)
                rows = rows[:, 2 * half : 2 * half + 2, :]
            else:
                first = 512 * int(group[2])
                rows = context[int(group[1]), first : first + 512, :].rearrange("(p c) e -> p c e", c=4)
                rows = rows[:, 2 * half : 2 * half + 2, :]
            nc.sync.dma_start(
                out=raw[group][:, 2 * FEATURES * half : 2 * FEATURES * (half + 1)].rearrange("p (n k) -> p n k", n=2),
                in_=rows,
            )

        def keep_warm(columns, count):
            unread = sums.tile([P, BANK], F32, name="unread", tag="acc")
            for repeat in range(count):
                nc.tensor.matmul(
                    out=unread[:, 0:columns], lhsT=blank[:, 0:P], rhs=blank[:, 0:columns], start=True, stop=True
                )

        def prepare(group, half, vector_helps):
            words = raw[group][:].bitcast(F32)
            for k_pass in range(2):
                if half == 0:
                    grouped[(group, k_pass)] = staging.tile([P, 4 * BANK], BF16, name="grouped", align_bytes=64)
                bank = turned.tile([P, BANK], F32, name="bank")
                for a in range(2):
                    for u in range(2):
                        first = 512 * (2 * half + a) + 256 * k_pass
                        nc.tensor.transpose(
                            bank[:, (2 * a + u) * P : (2 * a + u + 1) * P],
                            words[:, first + u : first + 2 * P : 2],
                            identity[:],
                        )
                target = grouped[(group, k_pass)][:].bitcast(F32)[:, BANK * half : BANK * (half + 1)]
                target = target.rearrange("p (a r u) -> p a r u", a=2, u=2)
                source = bank[:].rearrange("p (a u r) -> p a r u", a=2, u=2)
                if vector_helps and k_pass == 1:
                    nc.vector.tensor_copy(out=target, in_=source)
                else:
                    nc.scalar.copy(out=target, in_=source)

        def quantise(operand, values):
            width = values.shape[1] // 4
            codes[operand] = packed.tile([P, width], U32, name="codes_%s_%d_%d" % operand, align_bytes=64)
            scales[operand] = packed.tile([P, width], U8, name="scales_%s_%d_%d" % operand, align_bytes=64)
            nc.vector.quantize_mx(out=codes[operand][:].bitcast(FP8X4), scales=scales[operand][:], in_=values)

        def quantise_group(group):
            for k_pass in range(2):
                quantise((group, k_pass, 0), grouped[(group, k_pass)][:])

        def multiply(acc, stationary, stationary_columns, moving, moving_columns, k_pass):
            nc.tensor.matmul_mx(
                out=acc,
                lhsT=codes[stationary][:, stationary_columns].bitcast(FP8X4),
                lhsT_scale=scales[stationary][:, stationary_columns],
                rhs=codes[moving][:, moving_columns].bitcast(FP8X4),
                rhs_scale=scales[moving][:, moving_columns],
                start=(k_pass == 0),
                stop=(k_pass == 1),
            )

        def make_mask_row():
            nc.vector.tensor_scalar(out=mask_rows[0:1, :], in0=bits_row[:], scalar1=-1.0, scalar2=None, op0=ALU.add)

        def spread_mask():
            for b in range(2):
                mask_bank[b] = sums.tile([P, CONTEXT_ROWS], BF16, name="mask_bank", tag="acc")
                for h in range(2):
                    first = CONTEXT_ROWS * b + BANK * h
                    nc.tensor.matmul(
                        out=mask_bank[b][:, BANK * h : BANK * (h + 1)],
                        lhsT=ones[:],
                        rhs=mask_rows[:, first : first + BANK],
                        start=True,
                        stop=True,
                    )

        def copy_mask(b, on_vector):
            target = mask[:, CONTEXT_ROWS * b : CONTEXT_ROWS * (b + 1)]
            if on_vector:
                nc.vector.tensor_copy(out=target, in_=mask_bank[b][:])
            else:
                nc.scalar.copy(out=target, in_=mask_bank[b][:])

        def project_on_vector(b, e_pass, half):
            if half == 0:
                q_grouped[(b, e_pass)] = staging.tile([P, 4 * BANK], BF16, name="q_grouped", bufs=4, align_bytes=64)
            query_tiles = (2 * half, 2 * half + 1)
            acc = {}
            for n in query_tiles:
                acc[n] = sums.tile([P, BANK], F32, name="acc")
                for t in range(4):
                    for d_pass in range(2):
                        multiply(
                            acc[n][:, P * t : P * (t + 1)],
                            ("w%d" % e_pass, d_pass, 0), slice(P * t, P * (t + 1)),
                            ("q%d" % b, d_pass, 0), slice(P * n, P * (n + 1)),
                            d_pass,
                        )
            for n in query_tiles:
                nc.vector.tensor_tensor(
                    out=q_grouped[(b, e_pass)][:, BANK * n : BANK * (n + 1)].rearrange("p (i t) -> p i t", t=4),
                    in0=acc[n][:].rearrange("p (t i) -> p i t", t=4),
                    in1=bias[:, 4 * e_pass : 4 * e_pass + 4].unsqueeze(1).to_broadcast([P, P, 4]),
                    op=ALU.add,
                )
            for n in query_tiles:
                quantise(("z%d" % b, e_pass, n), q_grouped[(b, e_pass)][:, BANK * n : BANK * (n + 1)])
                q_words[(b, e_pass, n)] = (("z%d" % b, e_pass, n), slice(0, P))

        def project_on_scalar(b, e_pass):
            q_planes[(b, e_pass)] = staging.tile([P, 4 * BANK], BF16, name="q_planes", bufs=2)
            q_grouped[(b, e_pass)] = staging.tile([P, 4 * BANK], BF16, name="q_grouped", bufs=4, align_bytes=64)
            for t in range(4):
                acc = sums.tile([P, BANK], F32, name="acc")
                for d_pass in range(2):
                    multiply(
                        acc[:],
                        ("w%d" % e_pass, d_pass, 0), slice(P * t, P * (t + 1)),
                        ("q%d" % b, d_pass, 0), slice(0, BANK),
                        d_pass,
                    )
                nc.scalar.activation(
                    out=q_planes[(b, e_pass)][:, BANK * t : BANK * (t + 1)],
                    in_=acc[:],
                    func=ACT.Identity,
                    bias=bias[:, 4 * e_pass + t : 4 * e_pass + t + 1],
                    scale=1.0,
                )
            planes = q_planes[(b, e_pass)][:].rearrange("p (t i) -> p t i", t=4)
            for half in range(2):
                target = q_grouped[(b, e_pass)][:, 2 * BANK * half : 2 * BANK * (half + 1)]
                nc.gpsimd.tensor_scalar(
                    out=target.rearrange("p (m f t) -> p m t f", f=4, t=4),
                    in0=planes[:, :, 2 * P * half : 2 * P * (half + 1)].rearrange("p t (m f) -> p m t f", f=4),
                    scalar1=1.0,
                    scalar2=0.0,
                    op0=ALU.mult,
                    op1=ALU.add,
                )

        def quantise_q(b, e_pass):
            for half in range(2):
                operand = ("z%d" % b, e_pass, half)
                quantise(operand, q_grouped[(b, e_pass)][:, 2 * BANK * half : 2 * BANK * (half + 1)])
                for a in range(2):
                    q_words[(b, e_pass, 2 * half + a)] = (operand, slice(P * a, P * (a + 1)))

        def scores(b, n, before):
            score[(b, n)] = soft.tile([P, CONTEXT_ROWS], F32, name="score")
            for h in range(2):
                if h == 1 and before is not None:
                    row_maximum(before[0], before[1])
                acc = sums.tile([P, BANK], F32, name="acc")
                for e_pass in range(2):
                    operand, columns = q_words[(b, e_pass, n)]
                    multiply(acc[:], operand, columns, ("c%d%d" % (b, h), e_pass, 0), slice(0, BANK), e_pass)
                first = CONTEXT_ROWS * b + BANK * h
                nc.vector.scalar_tensor_tensor(
                    out=score[(b, n)][:, BANK * h : BANK * (h + 1)].rearrange("p (r c) -> p r c", c=4),
                    in0=mask[:, first : first + BANK].rearrange("p (r c) -> p r c", c=4),
                    scalar=penalty[:, 4 * b + n : 4 * b + n + 1],
                    in1=acc[:].rearrange("p (c r) -> p r c", c=4),
                    op0=ALU.mult,
                    op1=ALU.add,
                )

        def row_maximum(b, n):
            negative_max[(b, n)] = stats.tile([P, 1], F32, name="negative_max")
            nc.vector.tensor_reduce(
                out=negative_max[(b, n)][:], in_=score[(b, n)][:], axis=AX.X, op=ALU.max, negate=True
            )

        def exponentials(b, n):
            row_sum[(b, n)] = stats.tile([P, 1], F32, name="row_sum")
            nc.scalar.activation(
                out=score[(b, n)][:],
                in_=score[(b, n)][:],
                func=ACT.Exp,
                bias=negative_max[(b, n)][:],
                scale=1.0,
                accum_out=row_sum[(b, n)][:],
            )

        def reciprocal(b, n):
            inverse_sum[(b, n)] = stats.tile([P, 1], F32, name="inverse_sum")
            nc.vector.reciprocal(inverse_sum[(b, n)][:], row_sum[(b, n)][:])

        def normalise_and_store(b, n, on_vector, pieces=1):
            width = CONTEXT_ROWS // pieces
            for piece in range(pieces):
                weights = score[(b, n)][:, width * piece : width * (piece + 1)]
                inverse = inverse_sum[(b, n)][:]
                if on_vector:
                    nc.vector.tensor_scalar(out=weights, in0=weights, scalar1=inverse, scalar2=None, op0=ALU.mult)
                else:
                    nc.gpsimd.tensor_scalar(
                        out=weights, in0=weights, scalar1=inverse, scalar2=0.0, op0=ALU.mult, op1=ALU.add
                    )
                target = out[b].rearrange("(p n) j -> p n j", n=4)[:, n, width * piece : width * (piece + 1)]
                nc.sync.dma_start(out=target, in_=weights)

        for group in GROUPS:
            for half in range(2):
                load(group, half)
                if (group, half) == ("q0", 0):
                    nc.sync.dma_start(out=bits_row[:], in_=context_bit.rearrange("(o b) j -> o (b j)", o=1))
                if (group, half) == ("w0", 1):
                    nc.sync.dma_start(
                        out=bias_bf16[:].rearrange("p (g t) -> p g t", g=2),
                        in_=b_in.rearrange("(g p t) -> p g t", g=2, t=4),
                    )
                    nc.sync.dma_start(
                        out=query_bits[:].rearrange("p (b n) -> p b n", b=2),
                        in_=query_bit.rearrange("b (p n) -> p b n", n=4),
                    )

        make_mask_row()
        keep_warm(BANK, 6)
        prepare("q0", 0, True)
        prepare("q0", 1, True)
        spread_mask()
        quantise_group("q0")
        copy_mask(0, True)
        prepare("w0", 0, True)
        keep_warm(BANK // 2, 1)
        prepare("w0", 1, False)
        keep_warm(BANK // 2, 1)
        quantise_group("w0")
        prepare("w1", 0, True)
        keep_warm(BANK // 2, 1)
        prepare("w1", 1, True)
        quantise_group("w1")
        copy_mask(1, False)
        nc.vector.tensor_copy(out=bias[:], in_=bias_bf16[:])

        project_on_vector(0, 0, 0)
        project_on_vector(0, 0, 1)
        prepare("c00", 0, False)
        keep_warm(BANK // 2, 1)
        prepare("c00", 1, False)
        project_on_vector(0, 1, 0)
        quantise_group("c00")
        prepare("c01", 0, False)
        keep_warm(BANK // 2, 1)
        prepare("c01", 1, False)
        project_on_vector(0, 1, 1)
        quantise_group("c01")
        prepare("q1", 0, False)
        keep_warm(BANK // 2, 1)
        prepare("q1", 1, False)
        keep_warm(BANK // 2, 1)
        prepare("c10", 0, False)
        quantise_group("q1")
        nc.vector.tensor_scalar(out=penalty[:], in0=query_bits[:], scalar1=MASKED, scalar2=None, op0=ALU.mult)

        scores(0, 0, None)
        row_maximum(0, 0)
        prepare("c10", 1, False)
        scores(0, 1, None)
        row_maximum(0, 1)
        quantise_group("c10")
        project_on_scalar(1, 0)
        exponentials(0, 0)
        scores(0, 2, None)
        row_maximum(0, 2)
        quantise_q(1, 0)
        reciprocal(0, 0)
        project_on_scalar(1, 1)
        exponentials(0, 1)
        scores(0, 3, None)
        row_maximum(0, 3)
        reciprocal(0, 1)
        quantise_q(1, 1)
        prepare("c11", 0, False)
        keep_warm(BANK // 2, 1)
        prepare("c11", 1, False)
        quantise_group("c11")
        exponentials(0, 2)
        exponentials(0, 3)
        reciprocal(0, 2)
        for n in range(3):
            normalise_and_store(0, n, False)

        before = (0, 3)
        scores(1, 0, None)
        for n in range(4):
            if n < 3:
                scores(1, n + 1, (1, n))
            else:
                row_maximum(1, 3)
            exponentials(1, n)
            reciprocal(before[0], before[1])
            normalise_and_store(before[0], before[1], n == 3)
            before = (1, n)
        reciprocal(before[0], before[1])
        normalise_and_store(before[0], before[1], True, 2)
